import numpy as np
import ml_dtypes


def mxq(x, axis, fmt="e4m3"):
    dtype, down = {"e4m3": (ml_dtypes.float8_e4m3fn, 7), "e5m2": (ml_dtypes.float8_e5m2, 14)}[fmt]
    v = np.moveaxis(np.asarray(x, np.float32).astype(ml_dtypes.bfloat16).astype(np.float64), axis, -1)
    blocks = v.reshape(v.shape[:-1] + (-1, 32))
    amax = np.abs(blocks).max(-1, keepdims=True)
    byte = np.maximum(np.where(amax > 0, np.frexp(amax)[1] - 1 + 127, 0) - down, 1)
    scale = np.exp2(byte - 127.0)
    codes = (blocks / scale).astype(np.float32).astype(dtype).astype(np.float64)
    return np.moveaxis((codes * scale).reshape(v.shape), -1, axis)


WIDE = False


def mx_kscale(k):
    if not WIDE:
        return np.ones(k)
    levels = np.array([10, -10, 5, -5, 0])
    if k % 512:
        return np.exp2(np.random.permutation(np.resize(levels, k // 32))).repeat(32)
    a = np.empty((k // 512, 16))
    for p in range(k // 512):
        a[p, :8] = np.random.permutation(np.resize(levels, 8))
        for g in range(8):
            far = levels[np.abs(levels - a[p, g]) >= 10]
            a[p, g + 8] = far[np.random.randint(len(far))]
    return np.exp2(a.ravel()).repeat(32)


BF16 = ml_dtypes.bfloat16


def bf(x):
    return np.asarray(x, np.float32).astype(BF16)


def f64(x):
    return np.asarray(x).astype(np.float64)


S, E, C, HD, HP = 2048, 768, 256, 512, 8192
R = 2 * HP


def sigmoid(v):
    return 1.0 / (1.0 + np.exp(-v))


def setup_inputs():
    s, t = mx_kscale(R), mx_kscale(HD)
    return {"r": bf(np.abs(np.random.standard_normal((C, R))) * 0.5 * s),
            "psi_w1": bf(np.random.standard_normal((HD, R)) * 2.0 / np.sqrt(R) / s * t[:, None]),
            "psi_b1": bf(np.random.standard_normal(HD) * 0.3 * t),
            "w_dw": bf(np.random.standard_normal((E, HD)) * 1.5 / np.sqrt(HD) / t),
            "b_dw": bf(np.random.standard_normal(E) * 0.3),
            "w_gate": bf(np.random.standard_normal((E, HD)) * 1.5 / np.sqrt(HD) / t),
            "b_gate": bf(np.random.standard_normal(E) * 0.3),
            "W0": bf(np.random.standard_normal(E) * 0.1)}


def reference(r, psi_w1, psi_b1, w_dw, b_dw, w_gate, b_gate, W0):
    hid = np.maximum((mxq(f64(r), 1, "e4m3") @ mxq(f64(psi_w1), 1, "e4m3").T) + f64(psi_b1), 0.0)
    hq = mxq(hid, 1, "e4m3")
    dW = (hq @ mxq(f64(w_dw), 1, "e4m3").T) + f64(b_dw)
    gate = sigmoid((hq @ mxq(f64(w_gate), 1, "e4m3").T) + f64(b_gate))
    return f64(W0)[None, :] + gate * dW

@@ -1,0 +1,263 @@
+from contextlib import ExitStack
+
+import concourse.mybir as mybir
+from concourse.masks import make_identity
+
+F32 = mybir.dt.float32
+BF16 = mybir.dt.bfloat16
+U32 = mybir.dt.uint32
+U8 = mybir.dt.uint8
+FP8X4 = mybir.dt.float8_e4m3fn_x4
+ACT = mybir.ActivationFunctionType
+ALU = mybir.AluOpType
+
+P = 128
+PACK = 4
+K_PASS = P * PACK
+WORDS_PASS = K_PASS // 2
+
+CLASSES, R, HD, E = 256, 16384, 512, 768
+PASSES = R // K_PASS
+CLASS_SETS = CLASSES // P
+HD_SETS = HD // P
+ROW_SETS = CLASS_SETS + HD_SETS
+E_SETS = E // P
+E_PAIRS = E_SETS // 2
+
+CHUNK_PASSES = 2
+CHUNK_K = CHUNK_PASSES * K_PASS
+CHUNKS = PASSES // CHUNK_PASSES
+RAW_BUFS = 8
+RUN = 1
+ROUNDS = PASSES // RUN
+PREP_PASS = RAW_BUFS * CHUNK_PASSES
+
+FLOPS = 2 * CLASSES * R * HD + 2 * 2 * CLASSES * HD * E
+
+
+def tile_metalinearheadml_pb_k_kernel(tc, r, psi_w1, psi_b1, w_dw, b_dw, w_gate, b_gate, W0, out):
+    nc = tc.nc
+    with ExitStack() as stack:
+        consts = stack.enter_context(tc.tile_pool(name="consts", bufs=1))
+        raw_pool = stack.enter_context(tc.tile_pool(name="raw", bufs=RAW_BUFS))
+        grouped_pool = stack.enter_context(tc.tile_pool(name="grouped", bufs=2 * RUN + 2))
+        codes_pool = stack.enter_context(tc.tile_pool(name="codes", bufs=3 * RUN + 2))
+        tail_pool = stack.enter_context(tc.tile_pool(name="tail", bufs=E_SETS))
+        banks = stack.enter_context(tc.psum_pool(name="banks", bufs=4))
+        accs = stack.enter_context(tc.psum_pool(name="accs", bufs=1))
+        stack.enter_context(tc.manual_schedule())
+
+        ident = consts.tile([P, P], F32)
+        make_identity(nc, ident[:])
+        ones = consts.tile([P, P], BF16)
+        nc.vector.memset(ones[:], 1.0)
+
+        bias_rows = consts.tile([P, HD], BF16)
+        nc.vector.memset(bias_rows[:], 0.0)
+        nc.scalar.dma_start(out=bias_rows[0:1, :], in_=psi_b1.rearrange("(o c) -> o c", o=1))
+        nc.scalar.dma_start(out=bias_rows[1:4, 0 : 2 * P], in_=b_gate.rearrange("(v c) -> v c", c=2 * P))
+        nc.scalar.dma_start(out=bias_rows[4:7, 0 : 2 * P], in_=b_dw.rearrange("(v c) -> v c", c=2 * P))
+        w0_rows = consts.tile([P, E], BF16)
+        nc.vector.memset(w0_rows[:], 0.0)
+        nc.scalar.dma_start(out=w0_rows[0:1, :], in_=W0.rearrange("(o c) -> o c", o=1))
+        warm = consts.tile([P, 2], F32)
+        nc.vector.memset(warm[:], 0.0)
+        nc.scalar.activation(out=warm[:, 1:2], in_=warm[:, 0:1], func=ACT.Sigmoid)
+
+        r_rows = r.rearrange("(s p) k -> p s k", p=P)
+        w1_rows = psi_w1.rearrange("(p t) k -> p t k", t=HD_SETS)
+
+        def load_chunk(c):
+            raw = raw_pool.tile([P, ROW_SETS, CHUNK_K], BF16)
+            pieces = CHUNK_PASSES if c == CHUNKS - 1 else 1
+            width = CHUNK_K // pieces
+            for piece in range(pieces):
+                cols = slice(piece * width, (piece + 1) * width)
+                k = slice(c * CHUNK_K + piece * width, c * CHUNK_K + (piece + 1) * width)
+                nc.sync.dma_start(out=raw[:, 0:CLASS_SETS, cols], in_=r_rows[:, :, k])
+                for u in range(2):
+                    first = CLASS_SETS + 2 * u
+                    nc.sync.dma_start(out=raw[:, first : first + 2, cols], in_=w1_rows[:, 2 * u : 2 * u + 2, k])
+            return raw
+
+        raw_chunks = {}
+        for c in range(RAW_BUFS):
+            raw_chunks[c] = load_chunk(c)
+
+        w2_raw = consts.tile([P, 2 * E_SETS, HD], BF16)
+        nc.sync.dma_start(
+            out=w2_raw[:, 0:E_SETS, :].rearrange("p (v e) k -> p v (e k)", e=2),
+            in_=w_gate.rearrange("(v p e) k -> p v (e k)", p=P, e=2),
+        )
+        nc.sync.dma_start(
+            out=w2_raw[:, E_SETS : 2 * E_SETS, :].rearrange("p (v e) k -> p v (e k)", e=2),
+            in_=w_dw.rearrange("(v p e) k -> p v (e k)", p=P, e=2),
+        )
+        B1_COL, BGATE_COL, BDW_COL = 0, 4, 10
+
+        def transpose_pair(words, grouped, copy):
+            bank = banks.tile([P, 2, 2, P], F32, tag="bank")
+            for s in range(2):
+                for u in range(2):
+                    nc.tensor.transpose(bank[:, s, u, :], words[:, s, u : WORDS_PASS : 2], ident[:])
+            copy(out=grouped.bitcast(F32), in_=bank[:].rearrange("p s u m -> p s m u"))
+
+        hid_acc = [accs.tile([P, CLASSES], F32, name="acc%d" % t, tag="acc%d" % t) for t in range(HD_SETS)]
+        grouped_of = {}
+        codes_of = {}
+
+        def transpose_pass(g):
+            words = raw_chunks[g // CHUNK_PASSES][:].bitcast(F32)
+            cols = slice((g % CHUNK_PASSES) * WORDS_PASS, (g % CHUNK_PASSES + 1) * WORDS_PASS)
+            r_grouped = grouped_pool.tile([P, CLASS_SETS, P, PACK], BF16, align_bytes=64)
+            w_grouped = grouped_pool.tile([P, HD_SETS, P, PACK], BF16, align_bytes=64)
+            transpose_pair(words[:, 0:2, cols], r_grouped[:], nc.vector.tensor_copy)
+            transpose_pair(words[:, 2:4, cols], w_grouped[:, 0:2], nc.scalar.copy)
+            transpose_pair(words[:, 4:6, cols], w_grouped[:, 2:4], nc.scalar.copy)
+            grouped_of[g] = (r_grouped, w_grouped)
+
+        def quantise_pass(g):
+            r_grouped, w_grouped = grouped_of[g]
+            r_codes = codes_pool.tile([P, CLASSES], U32, align_bytes=64)
+            r_scales = codes_pool.tile([P, CLASSES], U8, align_bytes=64)
+            w_codes = codes_pool.tile([P, HD], U32, align_bytes=64)
+            w_scales = codes_pool.tile([P, HD], U8, align_bytes=64)
+            nc.vector.quantize_mx(
+                out=r_codes[:].bitcast(FP8X4), scales=r_scales[:], in_=r_grouped[:].rearrange("p s m t -> p (s m t)")
+            )
+            nc.vector.quantize_mx(
+                out=w_codes[:].bitcast(FP8X4), scales=w_scales[:], in_=w_grouped[:].rearrange("p s m t -> p (s m t)")
+            )
+            codes_of[g] = (r_codes, r_scales, w_codes, w_scales)
+
+        def multiply_pass(g):
+            r_codes, r_scales, w_codes, w_scales = codes_of[g]
+            for t in range(HD_SETS):
+                units = slice(t * P, (t + 1) * P)
+                nc.tensor.matmul_mx(
+                    out=hid_acc[t][:],
+                    lhsT=w_codes[:, units].bitcast(FP8X4),
+                    lhsT_scale=w_scales[:, units],
+                    rhs=r_codes[:].bitcast(FP8X4),
+                    rhs_scale=r_scales[:],
+                    start=(g == 0),
+                    stop=(g == PASSES - 1),
+                )
+
+        w2_codes = consts.tile([P, 2 * E_SETS * P], U32, align_bytes=64)
+        w2_scales = consts.tile([P, 2 * E_SETS * P], U8, align_bytes=64)
+        w2_grouped = consts.tile([P, 2 * E_SETS, P, PACK], BF16, align_bytes=64)
+        bias_cols = consts.tile([P, 16], F32)
+        w0_all = consts.tile([P, E], F32)
+
+        def spread_small_operands():
+            bias_bank = banks.tile([P, 4, P], F32, tag="bank")
+            bias_words = bias_rows[:].bitcast(F32)
+            for u in range(2):
+                nc.tensor.transpose(bias_bank[:, u, :], bias_words[:, u : 2 * P : 2], ident[:])
+            nc.tensor.transpose(bias_bank[:, 2, :], bias_words[:, 0:P], ident[:])
+            for u in range(2):
+                first = B1_COL + 2 * u
+                nc.vector.tensor_copy(out=bias_cols[:, first : first + 2], in_=bias_bank[:, u, 0:1].bitcast(BF16))
+            nc.vector.tensor_copy(out=bias_cols[:, BGATE_COL:16], in_=bias_bank[:, 2, 1:7].bitcast(BF16))
+            for first, width in ((0, 512), (512, 256)):
+                w0_bank = banks.tile([P, 4 * P], F32, tag="bank")
+                nc.tensor.matmul(
+                    out=w0_bank[:, 0:width], lhsT=ones[:], rhs=w0_rows[:, first : first + width], start=True, stop=True
+                )
+                nc.scalar.copy(out=w0_all[:, first : first + width], in_=w0_bank[:, 0:width])
+
+        def prepare_second_stage():
+            w2_words = w2_raw[:].bitcast(F32)
+            for pair in range(E_SETS):
+                sets = slice(2 * pair, 2 * pair + 2)
+                copy = nc.vector.tensor_copy if pair % 3 == 0 else nc.scalar.copy
+                transpose_pair(w2_words[:, sets, :], w2_grouped[:, sets], copy)
+            flat = w2_grouped[:].rearrange("p s m t -> p (s m t)")
+            for first, sets in ((0, 8), (8, 4)):
+                cols = slice(first * P, (first + sets) * P)
+                nc.vector.quantize_mx(
+                    out=w2_codes[:, cols].bitcast(FP8X4),
+                    scales=w2_scales[:, cols],
+                    in_=flat[:, first * K_PASS : (first + sets) * K_PASS],
+                )
+
+        for i in range(ROUNDS + 2):
+            for g in range(i * RUN, (i + 1) * RUN):
+                if g == PREP_PASS:
+                    prepare_second_stage()
+                if g < PASSES:
+                    transpose_pass(g)
+                    last_of_chunk = g % CHUNK_PASSES == CHUNK_PASSES - 1
+                    if last_of_chunk and g // CHUNK_PASSES + RAW_BUFS < CHUNKS:
+                        raw_chunks[g // CHUNK_PASSES + RAW_BUFS] = load_chunk(g // CHUNK_PASSES + RAW_BUFS)
+                if g == CHUNK_PASSES - 1:
+                    spread_small_operands()
+                if 0 <= g - RUN < PASSES:
+                    quantise_pass(g - RUN)
+            for g in range((i - 2) * RUN, (i - 1) * RUN):
+                if 0 <= g:
+                    multiply_pass(g)
+
+        hid_planes = consts.tile([P, HD_SETS, CLASSES], BF16)
+        for t in range(HD_SETS):
+            bias = bias_cols[:, B1_COL + t : B1_COL + t + 1]
+            if t % 2 == 0:
+                nc.scalar.activation(out=hid_planes[:, t, :], in_=hid_acc[t][:], func=ACT.Relu, bias=bias, scale=1.0)
+            else:
+                nc.vector.tensor_scalar(
+                    out=hid_planes[:, t, :], in0=hid_acc[t][:], scalar1=bias, scalar2=0.0, op0=ALU.add, op1=ALU.max
+                )
+        hid_grouped = consts.tile([P, CLASSES, PACK], BF16, align_bytes=64)
+        nc.vector.tensor_copy(out=hid_grouped[:], in_=hid_planes[:].rearrange("p t c -> p c t"))
+        hid_codes = consts.tile([P, CLASSES], U32, align_bytes=64)
+        hid_scales = consts.tile([P, CLASSES], U8, align_bytes=64)
+        nc.vector.quantize_mx(
+            out=hid_codes[:].bitcast(FP8X4), scales=hid_scales[:], in_=hid_grouped[:].rearrange("p c t -> p (c t)")
+        )
+
+        products = []
+        for j in range(E_SETS):
+            pre = banks.tile([P, 2, CLASSES], F32, tag="bank")
+            for plane in range(2):
+                outputs = slice((plane * E_SETS + j) * P, (plane * E_SETS + j + 1) * P)
+                nc.tensor.matmul_mx(
+                    out=pre[:, plane, :],
+                    lhsT=w2_codes[:, outputs].bitcast(FP8X4),
+                    lhsT_scale=w2_scales[:, outputs],
+                    rhs=hid_codes[:].bitcast(FP8X4),
+                    rhs_scale=hid_scales[:],
+                    start=True,
+                    stop=True,
+                )
+            gate = tail_pool.tile([P, CLASSES], F32)
+            nc.scalar.activation(
+                out=gate[:], in_=pre[:, 0, :], func=ACT.Sigmoid, bias=bias_cols[:, BGATE_COL + j : BGATE_COL + j + 1], scale=1.0
+            )
+            product = tail_pool.tile([P, CLASSES], F32)
+            nc.vector.scalar_tensor_tensor(
+                out=product[:],
+                in0=pre[:, 1, :],
+                scalar=bias_cols[:, BDW_COL + j : BDW_COL + j + 1],
+                in1=gate[:],
+                op0=ALU.add,
+                op1=ALU.mult,
+            )
+            products.append(product)
+
+        out_rows = out.rearrange("(c p) x -> p c x", p=P)
+        for v in range(E_PAIRS):
+            back = accs.tile([P, CLASS_SETS, 2, P], F32, name="back%d" % v, tag="acc%d" % v)
+            for e in range(2):
+                for c in range(CLASS_SETS):
+                    nc.tensor.transpose(back[:, c, e, :], products[2 * v + e][:, c * P : (c + 1) * P], ident[:])
+            result = tail_pool.tile([P, CLASS_SETS, 2 * P], F32, bufs=E_PAIRS)
+            outputs = slice(v * 2 * P, (v + 1) * 2 * P)
+            w0_pairs = w0_all[:, outputs].rearrange("p (m e) -> p m e", e=2)
+            nc.vector.tensor_tensor(
+                out=result[:].rearrange("p c (m e) -> p c m e", e=2),
+                in0=back[:].rearrange("p c e m -> p c m e"),
+                in1=w0_pairs.unsqueeze(1).to_broadcast([P, CLASS_SETS, P, 2]),
+                op=ALU.add,
+            )
+            nc.sync.dma_start(out=out_rows[:, :, outputs], in_=result[:])

@@ -40,6 +40,7 @@ def tile_metalinearheadml_pb_k_kernel(tc, r, psi_w1, psi_b1, w_dw, b_dw, w_gate,
     with ExitStack() as stack:
         consts = stack.enter_context(tc.tile_pool(name="consts", bufs=1))
         raw_pool = stack.enter_context(tc.tile_pool(name="raw", bufs=RAW_BUFS))
+        split_pool = stack.enter_context(tc.tile_pool(name="split", bufs=3))
         grouped_pool = stack.enter_context(tc.tile_pool(name="grouped", bufs=2 * RUN + 2))
         codes_pool = stack.enter_context(tc.tile_pool(name="codes", bufs=3 * RUN + 2))
         tail_pool = stack.enter_context(tc.tile_pool(name="tail", bufs=E_SETS))
@@ -95,25 +96,42 @@ def tile_metalinearheadml_pb_k_kernel(tc, r, psi_w1, psi_b1, w_dw, b_dw, w_gate,
         )
         B1_COL, BGATE_COL, BDW_COL = 0, 4, 10
 
-        def transpose_pair(words, grouped, copy):
+        def transpose_pair(half, grouped, copy):
             bank = banks.tile([P, 2, 2, P], F32, tag="bank")
             for s in range(2):
                 for u in range(2):
-                    nc.tensor.transpose(bank[:, s, u, :], words[:, s, u : WORDS_PASS : 2], ident[:])
+                    nc.tensor.transpose(bank[:, s, u, :], half(s, u), ident[:])
             copy(out=grouped.bitcast(F32), in_=bank[:].rearrange("p s u m -> p s m u"))
 
         hid_acc = [accs.tile([P, CLASSES], F32, name="acc%d" % t, tag="acc%d" % t) for t in range(HD_SETS)]
+        split_of = {}
         grouped_of = {}
         codes_of = {}
 
+        def split_pass(g):
+            first = (g % CHUNK_PASSES) * K_PASS
+            blocks = raw_chunks[g // CHUNK_PASSES][:, :, first : first + K_PASS].rearrange(
+                "p s (b u w) -> p u s b w", u=2, w=16
+            )
+            split = split_pool.tile([P, 2, ROW_SETS, WORDS_PASS], BF16, align_bytes=64)
+            for u in range(2):
+                nc.vector.tensor_copy(out=split[:, u].rearrange("p s (b w) -> p s b w", w=16), in_=blocks[:, u])
+            split_of[g] = split
+
         def transpose_pass(g):
-            words = raw_chunks[g // CHUNK_PASSES][:].bitcast(F32)
-            cols = slice((g % CHUNK_PASSES) * WORDS_PASS, (g % CHUNK_PASSES + 1) * WORDS_PASS)
+            words = split_of[g][:].rearrange("p u s k -> p (u s k)").bitcast(F32)
+
+            def half(s, u):
+                first = (u * ROW_SETS + s) * P
+                return words[:, first : first + P]
+
             r_grouped = grouped_pool.tile([P, CLASS_SETS, P, PACK], BF16, align_bytes=64)
             w_grouped = grouped_pool.tile([P, HD_SETS, P, PACK], BF16, align_bytes=64)
-            transpose_pair(words[:, 0:2, cols], r_grouped[:], nc.vector.tensor_copy)
-            transpose_pair(words[:, 2:4, cols], w_grouped[:, 0:2], nc.scalar.copy)
-            transpose_pair(words[:, 4:6, cols], w_grouped[:, 2:4], nc.scalar.copy)
+            transpose_pair(half, r_grouped[:], nc.scalar.copy)
+            for first in (0, 2):
+                transpose_pair(
+                    lambda s, u: half(CLASS_SETS + first + s, u), w_grouped[:, first : first + 2], nc.scalar.copy
+                )
             grouped_of[g] = (r_grouped, w_grouped)
 
         def quantise_pass(g):
@@ -170,9 +188,12 @@ def tile_metalinearheadml_pb_k_kernel(tc, r, psi_w1, psi_b1, w_dw, b_dw, w_gate,
         def prepare_second_stage():
             w2_words = w2_raw[:].bitcast(F32)
             for pair in range(E_SETS):
-                sets = slice(2 * pair, 2 * pair + 2)
                 copy = nc.vector.tensor_copy if pair % 3 == 0 else nc.scalar.copy
-                transpose_pair(w2_words[:, sets, :], w2_grouped[:, sets], copy)
+                transpose_pair(
+                    lambda s, u: w2_words[:, 2 * pair + s, u : WORDS_PASS : 2],
+                    w2_grouped[:, 2 * pair : 2 * pair + 2],
+                    copy,
+                )
             flat = w2_grouped[:].rearrange("p s m t -> p (s m t)")
             for first, sets in ((0, 8), (8, 4)):
                 cols = slice(first * P, (first + sets) * P)
@@ -182,19 +203,23 @@ def tile_metalinearheadml_pb_k_kernel(tc, r, psi_w1, psi_b1, w_dw, b_dw, w_gate,
                     in_=flat[:, first * K_PASS : (first + sets) * K_PASS],
                 )
 
+        split_pass(0)
         for i in range(ROUNDS + 2):
             for g in range(i * RUN, (i + 1) * RUN):
                 if g == PREP_PASS:
                     prepare_second_stage()
                 if g < PASSES:
                     transpose_pass(g)
-                    last_of_chunk = g % CHUNK_PASSES == CHUNK_PASSES - 1
-                    if last_of_chunk and g // CHUNK_PASSES + RAW_BUFS < CHUNKS:
-                        raw_chunks[g // CHUNK_PASSES + RAW_BUFS] = load_chunk(g // CHUNK_PASSES + RAW_BUFS)
                 if g == CHUNK_PASSES - 1:
                     spread_small_operands()
                 if 0 <= g - RUN < PASSES:
                     quantise_pass(g - RUN)
+                if g + 1 < PASSES:
+                    split_pass(g + 1)
+                    last_of_chunk = (g + 1) % CHUNK_PASSES == CHUNK_PASSES - 1
+                    c = (g + 1) // CHUNK_PASSES + RAW_BUFS
+                    if last_of_chunk and c < CHUNKS:
+                        raw_chunks[c] = load_chunk(c)
             for g in range((i - 2) * RUN, (i - 1) * RUN):
                 if 0 <= g:
                     multiply_pass(g)

@@ -30,6 +30,7 @@ CHUNKS = PASSES // CHUNK_PASSES
 RAW_BUFS = 8
 RUN = 1
 ROUNDS = PASSES // RUN
+SPLIT_AHEAD = 2
 PREP_PASS = RAW_BUFS * CHUNK_PASSES
 
 FLOPS = 2 * CLASSES * R * HD + 2 * 2 * CLASSES * HD * E
@@ -40,7 +41,7 @@ def tile_metalinearheadml_pb_k_kernel(tc, r, psi_w1, psi_b1, w_dw, b_dw, w_gate,
     with ExitStack() as stack:
         consts = stack.enter_context(tc.tile_pool(name="consts", bufs=1))
         raw_pool = stack.enter_context(tc.tile_pool(name="raw", bufs=RAW_BUFS))
-        split_pool = stack.enter_context(tc.tile_pool(name="split", bufs=3))
+        split_pool = stack.enter_context(tc.tile_pool(name="split", bufs=SPLIT_AHEAD + 2))
         grouped_pool = stack.enter_context(tc.tile_pool(name="grouped", bufs=2 * RUN + 2))
         codes_pool = stack.enter_context(tc.tile_pool(name="codes", bufs=3 * RUN + 2))
         tail_pool = stack.enter_context(tc.tile_pool(name="tail", bufs=E_SETS))
@@ -117,6 +118,10 @@ def tile_metalinearheadml_pb_k_kernel(tc, r, psi_w1, psi_b1, w_dw, b_dw, w_gate,
             for u in range(2):
                 nc.vector.tensor_copy(out=split[:, u].rearrange("p s (b w) -> p s b w", w=16), in_=blocks[:, u])
             split_of[g] = split
+            last_of_chunk = g % CHUNK_PASSES == CHUNK_PASSES - 1
+            c = g // CHUNK_PASSES + RAW_BUFS
+            if last_of_chunk and c < CHUNKS:
+                raw_chunks[c] = load_chunk(c)
 
         def transpose_pass(g):
             words = split_of[g][:].rearrange("p u s k -> p (u s k)").bitcast(F32)
@@ -203,7 +208,8 @@ def tile_metalinearheadml_pb_k_kernel(tc, r, psi_w1, psi_b1, w_dw, b_dw, w_gate,
                     in_=flat[:, first * K_PASS : (first + sets) * K_PASS],
                 )
 
-        split_pass(0)
+        for g in range(SPLIT_AHEAD):
+            split_pass(g)
         for i in range(ROUNDS + 2):
             for g in range(i * RUN, (i + 1) * RUN):
                 if g == PREP_PASS:
@@ -214,12 +220,9 @@ def tile_metalinearheadml_pb_k_kernel(tc, r, psi_w1, psi_b1, w_dw, b_dw, w_gate,
                     spread_small_operands()
                 if 0 <= g - RUN < PASSES:
                     quantise_pass(g - RUN)
-                if g + 1 < PASSES:
-                    split_pass(g + 1)
-                    last_of_chunk = (g + 1) % CHUNK_PASSES == CHUNK_PASSES - 1
-                    c = (g + 1) // CHUNK_PASSES + RAW_BUFS
-                    if last_of_chunk and c < CHUNKS:
-                        raw_chunks[c] = load_chunk(c)
+                ahead = g + SPLIT_AHEAD
+                if ahead < PASSES:
+                    split_pass(ahead)
             for g in range((i - 2) * RUN, (i - 1) * RUN):
                 if 0 <= g:
                     multiply_pass(g)

@@ -28,10 +28,8 @@ CHUNK_PASSES = 2
 CHUNK_K = CHUNK_PASSES * K_PASS
 CHUNKS = PASSES // CHUNK_PASSES
 RAW_BUFS = 8
-RUN = 1
-ROUNDS = PASSES // RUN
+AS_LOADED = 4
 SPLIT_AHEAD = 2
-PREP_PASS = RAW_BUFS * CHUNK_PASSES
 
 FLOPS = 2 * CLASSES * R * HD + 2 * 2 * CLASSES * HD * E
 
@@ -42,8 +40,8 @@ def tile_metalinearheadml_pb_k_kernel(tc, r, psi_w1, psi_b1, w_dw, b_dw, w_gate,
         consts = stack.enter_context(tc.tile_pool(name="consts", bufs=1))
         raw_pool = stack.enter_context(tc.tile_pool(name="raw", bufs=RAW_BUFS))
         split_pool = stack.enter_context(tc.tile_pool(name="split", bufs=SPLIT_AHEAD + 2))
-        grouped_pool = stack.enter_context(tc.tile_pool(name="grouped", bufs=2 * RUN + 2))
-        codes_pool = stack.enter_context(tc.tile_pool(name="codes", bufs=3 * RUN + 2))
+        grouped_pool = stack.enter_context(tc.tile_pool(name="grouped", bufs=4))
+        codes_pool = stack.enter_context(tc.tile_pool(name="codes", bufs=5))
         tail_pool = stack.enter_context(tc.tile_pool(name="tail", bufs=E_SETS))
         banks = stack.enter_context(tc.psum_pool(name="banks", bufs=4))
         accs = stack.enter_context(tc.psum_pool(name="accs", bufs=1))
@@ -54,6 +52,9 @@ def tile_metalinearheadml_pb_k_kernel(tc, r, psi_w1, psi_b1, w_dw, b_dw, w_gate,
         ones = consts.tile([P, P], BF16)
         nc.vector.memset(ones[:], 1.0)
 
+        warm = consts.tile([P, 2], F32)
+        nc.vector.memset(warm[:], 0.0)
+        nc.scalar.activation(out=warm[:, 1:2], in_=warm[:, 0:1], func=ACT.Sigmoid)
         bias_rows = consts.tile([P, HD], BF16)
         nc.vector.memset(bias_rows[:], 0.0)
         nc.scalar.dma_start(out=bias_rows[0:1, :], in_=psi_b1.rearrange("(o c) -> o c", o=1))
@@ -62,9 +63,6 @@ def tile_metalinearheadml_pb_k_kernel(tc, r, psi_w1, psi_b1, w_dw, b_dw, w_gate,
         w0_rows = consts.tile([P, E], BF16)
         nc.vector.memset(w0_rows[:], 0.0)
         nc.scalar.dma_start(out=w0_rows[0:1, :], in_=W0.rearrange("(o c) -> o c", o=1))
-        warm = consts.tile([P, 2], F32)
-        nc.vector.memset(warm[:], 0.0)
-        nc.scalar.activation(out=warm[:, 1:2], in_=warm[:, 0:1], func=ACT.Sigmoid)
 
         r_rows = r.rearrange("(s p) k -> p s k", p=P)
         w1_rows = psi_w1.rearrange("(p t) k -> p t k", t=HD_SETS)
@@ -82,27 +80,28 @@ def tile_metalinearheadml_pb_k_kernel(tc, r, psi_w1, psi_b1, w_dw, b_dw, w_gate,
                     nc.sync.dma_start(out=raw[:, first : first + 2, cols], in_=w1_rows[:, 2 * u : 2 * u + 2, k])
             return raw
 
+        w2_raw = consts.tile([P, 2 * E_SETS, HD], BF16)
+        for plane, weights in ((0, w_gate), (1, w_dw)):
+            rows = weights.rearrange("(v p e) k -> p v e k", p=P, e=2)
+            for v in range(E_PAIRS):
+                first = plane * E_SETS + 2 * v
+                nc.sync.dma_start(out=w2_raw[:, first : first + 2, :], in_=rows[:, v])
+
         raw_chunks = {}
         for c in range(RAW_BUFS):
             raw_chunks[c] = load_chunk(c)
 
-        w2_raw = consts.tile([P, 2 * E_SETS, HD], BF16)
-        nc.sync.dma_start(
-            out=w2_raw[:, 0:E_SETS, :].rearrange("p (v e) k -> p v (e k)", e=2),
-            in_=w_gate.rearrange("(v p e) k -> p v (e k)", p=P, e=2),
-        )
-        nc.sync.dma_start(
-            out=w2_raw[:, E_SETS : 2 * E_SETS, :].rearrange("p (v e) k -> p v (e k)", e=2),
-            in_=w_dw.rearrange("(v p e) k -> p v (e k)", p=P, e=2),
-        )
         B1_COL, BGATE_COL, BDW_COL = 0, 4, 10
 
         def transpose_pair(half, grouped, copy):
-            bank = banks.tile([P, 2, 2, P], F32, tag="bank")
+            bank = banks.tile([P, 2, 2 * P], F32, tag="bank")
             for s in range(2):
                 for u in range(2):
-                    nc.tensor.transpose(bank[:, s, u, :], half(s, u), ident[:])
-            copy(out=grouped.bitcast(F32), in_=bank[:].rearrange("p s u m -> p s m u"))
+                    nc.tensor.transpose(bank[:, u, s * P : (s + 1) * P], half(s, u), ident[:])
+            copy(
+                out=grouped.rearrange("p s m t -> p (s m t)").bitcast(F32).rearrange("p (c i u) -> p c u i", i=2, u=2),
+                in_=bank[:].rearrange("p u (c i) -> p c u i", i=2),
+            )
 
         hid_acc = [accs.tile([P, CLASSES], F32, name="acc%d" % t, tag="acc%d" % t) for t in range(HD_SETS)]
         split_of = {}
@@ -118,26 +117,35 @@ def tile_metalinearheadml_pb_k_kernel(tc, r, psi_w1, psi_b1, w_dw, b_dw, w_gate,
             for u in range(2):
                 nc.vector.tensor_copy(out=split[:, u].rearrange("p s (b w) -> p s b w", w=16), in_=blocks[:, u])
             split_of[g] = split
-            last_of_chunk = g % CHUNK_PASSES == CHUNK_PASSES - 1
+
+        def load_behind(g):
             c = g // CHUNK_PASSES + RAW_BUFS
-            if last_of_chunk and c < CHUNKS:
+            if g % CHUNK_PASSES == CHUNK_PASSES - 1 and c < CHUNKS:
                 raw_chunks[c] = load_chunk(c)
 
-        def transpose_pass(g):
-            words = split_of[g][:].rearrange("p u s k -> p (u s k)").bitcast(F32)
+        def transpose_rows(g, first, copy):
+            if g in split_of:
+                words = split_of[g][:].rearrange("p u s k -> p (u s k)").bitcast(F32)
 
-            def half(s, u):
-                first = (u * ROW_SETS + s) * P
-                return words[:, first : first + P]
+                def half(s, u):
+                    start = (u * ROW_SETS + first + s) * P
+                    return words[:, start : start + P]
 
-            r_grouped = grouped_pool.tile([P, CLASS_SETS, P, PACK], BF16, align_bytes=64)
-            w_grouped = grouped_pool.tile([P, HD_SETS, P, PACK], BF16, align_bytes=64)
-            transpose_pair(half, r_grouped[:], nc.scalar.copy)
-            for first in (0, 2):
-                transpose_pair(
-                    lambda s, u: half(CLASS_SETS + first + s, u), w_grouped[:, first : first + 2], nc.scalar.copy
-                )
-            grouped_of[g] = (r_grouped, w_grouped)
+            else:
+                words = raw_chunks[g // CHUNK_PASSES][:].bitcast(F32)
+                start = (g % CHUNK_PASSES) * WORDS_PASS
+
+                def half(s, u):
+                    return words[:, first + s, start + u : start + WORDS_PASS : 2]
+
+            if first == 0:
+                r_grouped = grouped_pool.tile([P, CLASS_SETS, P, PACK], BF16, align_bytes=64)
+                w_grouped = grouped_pool.tile([P, HD_SETS, P, PACK], BF16, align_bytes=64)
+                grouped_of[g] = (r_grouped, w_grouped)
+                transpose_pair(half, r_grouped[:], copy)
+            else:
+                w_grouped = grouped_of[g][1]
+                transpose_pair(half, w_grouped[:, first - CLASS_SETS : first - CLASS_SETS + 2], copy)
 
         def quantise_pass(g):
             r_grouped, w_grouped = grouped_of[g]
@@ -148,9 +156,15 @@ def tile_metalinearheadml_pb_k_kernel(tc, r, psi_w1, psi_b1, w_dw, b_dw, w_gate,
             nc.vector.quantize_mx(
                 out=r_codes[:].bitcast(FP8X4), scales=r_scales[:], in_=r_grouped[:].rearrange("p s m t -> p (s m t)")
             )
-            nc.vector.quantize_mx(
-                out=w_codes[:].bitcast(FP8X4), scales=w_scales[:], in_=w_grouped[:].rearrange("p s m t -> p (s m t)")
-            )
+            calls = 2 if g == PASSES - 1 else 1
+            sets = HD_SETS // calls
+            for call in range(calls):
+                cols = slice(call * sets * P, (call + 1) * sets * P)
+                nc.vector.quantize_mx(
+                    out=w_codes[:, cols].bitcast(FP8X4),
+                    scales=w_scales[:, cols],
+                    in_=w_grouped[:, call * sets : (call + 1) * sets].rearrange("p s m t -> p (s m t)"),
+                )
             codes_of[g] = (r_codes, r_scales, w_codes, w_scales)
 
         def multiply_pass(g):
@@ -193,7 +207,7 @@ def tile_metalinearheadml_pb_k_kernel(tc, r, psi_w1, psi_b1, w_dw, b_dw, w_gate,
         def prepare_second_stage():
             w2_words = w2_raw[:].bitcast(F32)
             for pair in range(E_SETS):
-                copy = nc.vector.tensor_copy if pair % 3 == 0 else nc.scalar.copy
+                copy = nc.vector.tensor_copy if pair % 2 == 0 else nc.scalar.copy
                 transpose_pair(
                     lambda s, u: w2_words[:, 2 * pair + s, u : WORDS_PASS : 2],
                     w2_grouped[:, 2 * pair : 2 * pair + 2],
@@ -208,24 +222,28 @@ def tile_metalinearheadml_pb_k_kernel(tc, r, psi_w1, psi_b1, w_dw, b_dw, w_gate,
                     in_=flat[:, first * K_PASS : (first + sets) * K_PASS],
                 )
 
-        for g in range(SPLIT_AHEAD):
-            split_pass(g)
-        for i in range(ROUNDS + 2):
-            for g in range(i * RUN, (i + 1) * RUN):
-                if g == PREP_PASS:
-                    prepare_second_stage()
-                if g < PASSES:
-                    transpose_pass(g)
-                if g == CHUNK_PASSES - 1:
-                    spread_small_operands()
-                if 0 <= g - RUN < PASSES:
-                    quantise_pass(g - RUN)
-                ahead = g + SPLIT_AHEAD
-                if ahead < PASSES:
-                    split_pass(ahead)
-            for g in range((i - 2) * RUN, (i - 1) * RUN):
-                if 0 <= g:
-                    multiply_pass(g)
+        prepare_second_stage()
+        for i in range(PASSES + 2):
+            last = i == PASSES - 1
+            if i < PASSES:
+                for first in (0, 2, 4):
+                    if last and first == 4:
+                        quantise_pass(i - 1)
+                        transpose_rows(i, first, nc.vector.tensor_copy)
+                    else:
+                        transpose_rows(i, first, nc.scalar.copy)
+                if i < AS_LOADED:
+                    load_behind(i)
+            if i == CHUNK_PASSES:
+                spread_small_operands()
+            if 0 <= i - 1 < PASSES and not last:
+                quantise_pass(i - 1)
+            ahead = i + SPLIT_AHEAD
+            if AS_LOADED <= ahead < PASSES - 1:
+                split_pass(ahead)
+                load_behind(ahead)
+            if 0 <= i - 2:
+                multiply_pass(i - 2)
 
         hid_planes = consts.tile([P, HD_SETS, CLASSES], BF16)
         for t in range(HD_SETS):

@@ -83,9 +83,12 @@ def tile_metalinearheadml_pb_k_kernel(tc, r, psi_w1, psi_b1, w_dw, b_dw, w_gate,
         w2_raw = consts.tile([P, 2 * E_SETS, HD], BF16)
         for plane, weights in ((0, w_gate), (1, w_dw)):
             rows = weights.rearrange("(v p e) k -> p v e k", p=P, e=2)
-            for v in range(E_PAIRS):
-                first = plane * E_SETS + 2 * v
-                nc.sync.dma_start(out=w2_raw[:, first : first + 2, :], in_=rows[:, v])
+            for v in (slice(0, 1), slice(1, E_PAIRS)) if plane == 0 else (slice(0, E_PAIRS),):
+                first = plane * E_SETS + 2 * v.start
+                nc.sync.dma_start(
+                    out=w2_raw[:, first : plane * E_SETS + 2 * v.stop, :].rearrange("p (v e) k -> p v (e k)", e=2),
+                    in_=rows[:, v].rearrange("p v e k -> p v (e k)"),
+                )
 
         raw_chunks = {}
         for c in range(RAW_BUFS):
@@ -185,7 +188,6 @@ def tile_metalinearheadml_pb_k_kernel(tc, r, psi_w1, psi_b1, w_dw, b_dw, w_gate,
         w2_scales = consts.tile([P, 2 * E_SETS * P], U8, align_bytes=64)
         w2_grouped = consts.tile([P, 2 * E_SETS, P, PACK], BF16, align_bytes=64)
         bias_cols = consts.tile([P, 16], F32)
-        w0_all = consts.tile([P, E], F32)
 
         def spread_small_operands():
             bias_bank = banks.tile([P, 4, P], F32, tag="bank")
@@ -197,12 +199,6 @@ def tile_metalinearheadml_pb_k_kernel(tc, r, psi_w1, psi_b1, w_dw, b_dw, w_gate,
                 first = B1_COL + 2 * u
                 nc.vector.tensor_copy(out=bias_cols[:, first : first + 2], in_=bias_bank[:, u, 0:1].bitcast(BF16))
             nc.vector.tensor_copy(out=bias_cols[:, BGATE_COL:16], in_=bias_bank[:, 2, 1:7].bitcast(BF16))
-            for first, width in ((0, 512), (512, 256)):
-                w0_bank = banks.tile([P, 4 * P], F32, tag="bank")
-                nc.tensor.matmul(
-                    out=w0_bank[:, 0:width], lhsT=ones[:], rhs=w0_rows[:, first : first + width], start=True, stop=True
-                )
-                nc.scalar.copy(out=w0_all[:, first : first + width], in_=w0_bank[:, 0:width])
 
         def prepare_second_stage():
             w2_words = w2_raw[:].bitcast(F32)
@@ -223,20 +219,14 @@ def tile_metalinearheadml_pb_k_kernel(tc, r, psi_w1, psi_b1, w_dw, b_dw, w_gate,
                 )
 
         prepare_second_stage()
+        spread_small_operands()
         for i in range(PASSES + 2):
-            last = i == PASSES - 1
             if i < PASSES:
                 for first in (0, 2, 4):
-                    if last and first == 4:
-                        quantise_pass(i - 1)
-                        transpose_rows(i, first, nc.vector.tensor_copy)
-                    else:
-                        transpose_rows(i, first, nc.scalar.copy)
+                    transpose_rows(i, first, nc.scalar.copy)
                 if i < AS_LOADED:
                     load_behind(i)
-            if i == CHUNK_PASSES:
-                spread_small_operands()
-            if 0 <= i - 1 < PASSES and not last:
+            if 0 <= i - 1 < PASSES:
                 quantise_pass(i - 1)
             ahead = i + SPLIT_AHEAD
             if AS_LOADED <= ahead < PASSES - 1:
@@ -255,15 +245,29 @@ def tile_metalinearheadml_pb_k_kernel(tc, r, psi_w1, psi_b1, w_dw, b_dw, w_gate,
                     out=hid_planes[:, t, :], in0=hid_acc[t][:], scalar1=bias, scalar2=0.0, op0=ALU.add, op1=ALU.max
                 )
         hid_grouped = consts.tile([P, CLASSES, PACK], BF16, align_bytes=64)
-        nc.vector.tensor_copy(out=hid_grouped[:], in_=hid_planes[:].rearrange("p t c -> p c t"))
+        by_class = hid_planes[:].rearrange("p t c -> p c t")
+        share = CLASSES * 3 // 4
+        nc.vector.tensor_copy(out=hid_grouped[:, 0:share], in_=by_class[:, 0:share])
+        nc.scalar.copy(out=hid_grouped[:, share:CLASSES], in_=by_class[:, share:CLASSES])
         hid_codes = consts.tile([P, CLASSES], U32, align_bytes=64)
         hid_scales = consts.tile([P, CLASSES], U8, align_bytes=64)
         nc.vector.quantize_mx(
             out=hid_codes[:].bitcast(FP8X4), scales=hid_scales[:], in_=hid_grouped[:].rearrange("p c t -> p (c t)")
         )
 
-        products = []
-        for j in range(E_SETS):
+        out_rows = out.rearrange("(c p) x -> p c x", p=P)
+        backs = []
+        for i, (v, class_sets) in enumerate(((0, (0, 1)), (1, (0, 1)), (2, (0,)), (2, (1,)))):
+            count = len(class_sets)
+            back = accs.tile([P, count, 2, P], F32, name="back%d" % i, tag="acc%d" % i)
+            w0_planes = w0_rows[:, v * 2 * P : (v + 1) * 2 * P].rearrange("p (m e) -> p e m", e=2)
+            for n in range(count):
+                nc.tensor.matmul(out=back[:, n], lhsT=ones[:], rhs=w0_planes, start=(n == 0), stop=False)
+            backs.append((v, class_sets, back))
+
+        products = {}
+
+        def multiply_outputs(j):
             pre = banks.tile([P, 2, CLASSES], F32, tag="bank")
             for plane in range(2):
                 outputs = slice((plane * E_SETS + j) * P, (plane * E_SETS + j + 1) * P)
@@ -289,21 +293,34 @@ def tile_metalinearheadml_pb_k_kernel(tc, r, psi_w1, psi_b1, w_dw, b_dw, w_gate,
                 op0=ALU.add,
                 op1=ALU.mult,
             )
-            products.append(product)
+            products[j] = product
 
-        out_rows = out.rearrange("(c p) x -> p c x", p=P)
-        for v in range(E_PAIRS):
-            back = accs.tile([P, CLASS_SETS, 2, P], F32, name="back%d" % v, tag="acc%d" % v)
-            for e in range(2):
-                for c in range(CLASS_SETS):
-                    nc.tensor.transpose(back[:, c, e, :], products[2 * v + e][:, c * P : (c + 1) * P], ident[:])
-            result = tail_pool.tile([P, CLASS_SETS, 2 * P], F32, bufs=E_PAIRS)
-            outputs = slice(v * 2 * P, (v + 1) * 2 * P)
-            w0_pairs = w0_all[:, outputs].rearrange("p (m e) -> p m e", e=2)
-            nc.vector.tensor_tensor(
-                out=result[:].rearrange("p c (m e) -> p c m e", e=2),
-                in0=back[:].rearrange("p c e m -> p c m e"),
-                in1=w0_pairs.unsqueeze(1).to_broadcast([P, CLASS_SETS, P, 2]),
-                op=ALU.add,
+        def turn_back(i):
+            v, class_sets, back = backs[i]
+            for n, c in enumerate(class_sets):
+                for e in range(2):
+                    nc.tensor.matmul(
+                        out=back[:, n, e, :],
+                        lhsT=products[2 * v + e][:, c * P : (c + 1) * P],
+                        rhs=ident[:],
+                        is_transpose=True,
+                        start=False,
+                        stop=(n == len(class_sets) - 1 and e == 1),
+                    )
+
+        def store(i):
+            v, class_sets, back = backs[i]
+            result = tail_pool.tile([P, len(class_sets), 2 * P], F32, name="result%d" % i, tag="result%d" % i, bufs=1)
+            copy = nc.scalar.copy if i % 2 == 0 else nc.vector.tensor_copy
+            copy(
+                out=result[:].rearrange("p c (m e) -> p c m e", e=2), in_=back[:].rearrange("p c e m -> p c m e")
             )
-            nc.sync.dma_start(out=out_rows[:, :, outputs], in_=result[:])
+            nc.sync.dma_start(
+                out=out_rows[:, class_sets[0] : class_sets[-1] + 1, v * 2 * P : (v + 1) * 2 * P], in_=result[:]
+            )
+
+        for j in range(E_SETS):
+            multiply_outputs(j)
+        for i in range(len(backs)):
+            turn_back(i)
+            store(i)

from contextlib import ExitStack

import concourse.mybir as mybir
from concourse.masks import make_identity

F32 = mybir.dt.float32
BF16 = mybir.dt.bfloat16
U32 = mybir.dt.uint32
U8 = mybir.dt.uint8
FP8X4 = mybir.dt.float8_e4m3fn_x4
ACT = mybir.ActivationFunctionType
ALU = mybir.AluOpType

P = 128
PACK = 4
K_PASS = P * PACK
WORDS_PASS = K_PASS // 2

CLASSES, R, HD, E = 256, 16384, 512, 768
PASSES = R // K_PASS
CLASS_SETS = CLASSES // P
HD_SETS = HD // P
ROW_SETS = CLASS_SETS + HD_SETS
E_SETS = E // P
E_PAIRS = E_SETS // 2

CHUNK_PASSES = 2
CHUNK_K = CHUNK_PASSES * K_PASS
CHUNKS = PASSES // CHUNK_PASSES
RAW_BUFS = 8
AS_LOADED = 4
SPLIT_AHEAD = 2

FLOPS = 2 * CLASSES * R * HD + 2 * 2 * CLASSES * HD * E


def tile_metalinearheadml_pb_k_kernel(tc, r, psi_w1, psi_b1, w_dw, b_dw, w_gate, b_gate, W0, out):
    nc = tc.nc
    with ExitStack() as stack:
        consts = stack.enter_context(tc.tile_pool(name="consts", bufs=1))
        raw_pool = stack.enter_context(tc.tile_pool(name="raw", bufs=RAW_BUFS))
        split_pool = stack.enter_context(tc.tile_pool(name="split", bufs=SPLIT_AHEAD + 2))
        grouped_pool = stack.enter_context(tc.tile_pool(name="grouped", bufs=4))
        codes_pool = stack.enter_context(tc.tile_pool(name="codes", bufs=5))
        tail_pool = stack.enter_context(tc.tile_pool(name="tail", bufs=E_SETS))
        banks = stack.enter_context(tc.psum_pool(name="banks", bufs=4))
        accs = stack.enter_context(tc.psum_pool(name="accs", bufs=1))
        stack.enter_context(tc.manual_schedule())

        ident = consts.tile([P, P], F32)
        make_identity(nc, ident[:])
        ones = consts.tile([P, P], BF16)
        nc.vector.memset(ones[:], 1.0)

        warm = consts.tile([P, 2], F32)
        nc.vector.memset(warm[:], 0.0)
        nc.scalar.activation(out=warm[:, 1:2], in_=warm[:, 0:1], func=ACT.Sigmoid)
        bias_rows = consts.tile([P, HD], BF16)
        nc.vector.memset(bias_rows[:], 0.0)
        nc.scalar.dma_start(out=bias_rows[0:1, :], in_=psi_b1.rearrange("(o c) -> o c", o=1))
        nc.scalar.dma_start(out=bias_rows[1:4, 0 : 2 * P], in_=b_gate.rearrange("(v c) -> v c", c=2 * P))
        nc.scalar.dma_start(out=bias_rows[4:7, 0 : 2 * P], in_=b_dw.rearrange("(v c) -> v c", c=2 * P))
        w0_rows = consts.tile([P, E], BF16)
        nc.vector.memset(w0_rows[:], 0.0)
        nc.scalar.dma_start(out=w0_rows[0:1, :], in_=W0.rearrange("(o c) -> o c", o=1))

        r_rows = r.rearrange("(s p) k -> p s k", p=P)
        w1_rows = psi_w1.rearrange("(p t) k -> p t k", t=HD_SETS)

        def load_chunk(c):
            raw = raw_pool.tile([P, ROW_SETS, CHUNK_K], BF16)
            pieces = CHUNK_PASSES if c == CHUNKS - 1 else 1
            width = CHUNK_K // pieces
            for piece in range(pieces):
                cols = slice(piece * width, (piece + 1) * width)
                k = slice(c * CHUNK_K + piece * width, c * CHUNK_K + (piece + 1) * width)
                nc.sync.dma_start(out=raw[:, 0:CLASS_SETS, cols], in_=r_rows[:, :, k])
                for u in range(2):
                    first = CLASS_SETS + 2 * u
                    nc.sync.dma_start(out=raw[:, first : first + 2, cols], in_=w1_rows[:, 2 * u : 2 * u + 2, k])
            return raw

        w2_raw = consts.tile([P, 2 * E_SETS, HD], BF16)
        for plane, weights in ((0, w_gate), (1, w_dw)):
            rows = weights.rearrange("(v p e) k -> p v e k", p=P, e=2)
            for v in (slice(0, 1), slice(1, E_PAIRS)) if plane == 0 else (slice(0, E_PAIRS),):
                first = plane * E_SETS + 2 * v.start
                nc.sync.dma_start(
                    out=w2_raw[:, first : plane * E_SETS + 2 * v.stop, :].rearrange("p (v e) k -> p v (e k)", e=2),
                    in_=rows[:, v].rearrange("p v e k -> p v (e k)"),
                )

        raw_chunks = {}
        for c in range(RAW_BUFS):
            raw_chunks[c] = load_chunk(c)

        B1_COL, BGATE_COL, BDW_COL = 0, 4, 10

        def transpose_pair(half, grouped, copy):
            bank = banks.tile([P, 2, 2 * P], F32, tag="bank")
            for s in range(2):
                for u in range(2):
                    nc.tensor.transpose(bank[:, u, s * P : (s + 1) * P], half(s, u), ident[:])
            copy(
                out=grouped.rearrange("p s m t -> p (s m t)").bitcast(F32).rearrange("p (c i u) -> p c u i", i=2, u=2),
                in_=bank[:].rearrange("p u (c i) -> p c u i", i=2),
            )

        hid_acc = [accs.tile([P, CLASSES], F32, name="acc%d" % t, tag="acc%d" % t) for t in range(HD_SETS)]
        split_of = {}
        grouped_of = {}
        codes_of = {}

        def split_pass(g):
            first = (g % CHUNK_PASSES) * K_PASS
            blocks = raw_chunks[g // CHUNK_PASSES][:, :, first : first + K_PASS].rearrange(
                "p s (b u w) -> p u s b w", u=2, w=16
            )
            split = split_pool.tile([P, 2, ROW_SETS, WORDS_PASS], BF16, align_bytes=64)
            for u in range(2):
                nc.vector.tensor_copy(out=split[:, u].rearrange("p s (b w) -> p s b w", w=16), in_=blocks[:, u])
            split_of[g] = split

        def load_behind(g):
            c = g // CHUNK_PASSES + RAW_BUFS
            if g % CHUNK_PASSES == CHUNK_PASSES - 1 and c < CHUNKS:
                raw_chunks[c] = load_chunk(c)

        def transpose_rows(g, first, copy):
            if g in split_of:
                words = split_of[g][:].rearrange("p u s k -> p (u s k)").bitcast(F32)

                def half(s, u):
                    start = (u * ROW_SETS + first + s) * P
                    return words[:, start : start + P]

            else:
                words = raw_chunks[g // CHUNK_PASSES][:].bitcast(F32)
                start = (g % CHUNK_PASSES) * WORDS_PASS

                def half(s, u):
                    return words[:, first + s, start + u : start + WORDS_PASS : 2]

            if first == 0:
                r_grouped = grouped_pool.tile([P, CLASS_SETS, P, PACK], BF16, align_bytes=64)
                w_grouped = grouped_pool.tile([P, HD_SETS, P, PACK], BF16, align_bytes=64)
                grouped_of[g] = (r_grouped, w_grouped)
                transpose_pair(half, r_grouped[:], copy)
            else:
                w_grouped = grouped_of[g][1]
                transpose_pair(half, w_grouped[:, first - CLASS_SETS : first - CLASS_SETS + 2], copy)

        def quantise_pass(g):
            r_grouped, w_grouped = grouped_of[g]
            r_codes = codes_pool.tile([P, CLASSES], U32, align_bytes=64)
            r_scales = codes_pool.tile([P, CLASSES], U8, align_bytes=64)
            w_codes = codes_pool.tile([P, HD], U32, align_bytes=64)
            w_scales = codes_pool.tile([P, HD], U8, align_bytes=64)
            nc.vector.quantize_mx(
                out=r_codes[:].bitcast(FP8X4), scales=r_scales[:], in_=r_grouped[:].rearrange("p s m t -> p (s m t)")
            )
            calls = 2 if g == PASSES - 1 else 1
            sets = HD_SETS // calls
            for call in range(calls):
                cols = slice(call * sets * P, (call + 1) * sets * P)
                nc.vector.quantize_mx(
                    out=w_codes[:, cols].bitcast(FP8X4),
                    scales=w_scales[:, cols],
                    in_=w_grouped[:, call * sets : (call + 1) * sets].rearrange("p s m t -> p (s m t)"),
                )
            codes_of[g] = (r_codes, r_scales, w_codes, w_scales)

        def multiply_pass(g):
            r_codes, r_scales, w_codes, w_scales = codes_of[g]
            for t in range(HD_SETS):
                units = slice(t * P, (t + 1) * P)
                nc.tensor.matmul_mx(
                    out=hid_acc[t][:],
                    lhsT=w_codes[:, units].bitcast(FP8X4),
                    lhsT_scale=w_scales[:, units],
                    rhs=r_codes[:].bitcast(FP8X4),
                    rhs_scale=r_scales[:],
                    start=(g == 0),
                    stop=(g == PASSES - 1),
                )

        w2_codes = consts.tile([P, 2 * E_SETS * P], U32, align_bytes=64)
        w2_scales = consts.tile([P, 2 * E_SETS * P], U8, align_bytes=64)
        w2_grouped = consts.tile([P, 2 * E_SETS, P, PACK], BF16, align_bytes=64)
        bias_cols = consts.tile([P, 16], F32)

        def spread_small_operands():
            bias_bank = banks.tile([P, 4, P], F32, tag="bank")
            bias_words = bias_rows[:].bitcast(F32)
            for u in range(2):
                nc.tensor.transpose(bias_bank[:, u, :], bias_words[:, u : 2 * P : 2], ident[:])
            nc.tensor.transpose(bias_bank[:, 2, :], bias_words[:, 0:P], ident[:])
            for u in range(2):
                first = B1_COL + 2 * u
                nc.vector.tensor_copy(out=bias_cols[:, first : first + 2], in_=bias_bank[:, u, 0:1].bitcast(BF16))
            nc.vector.tensor_copy(out=bias_cols[:, BGATE_COL:16], in_=bias_bank[:, 2, 1:7].bitcast(BF16))

        def prepare_second_stage():
            w2_words = w2_raw[:].bitcast(F32)
            for pair in range(E_SETS):
                copy = nc.vector.tensor_copy if pair % 2 == 0 else nc.scalar.copy
                transpose_pair(
                    lambda s, u: w2_words[:, 2 * pair + s, u : WORDS_PASS : 2],
                    w2_grouped[:, 2 * pair : 2 * pair + 2],
                    copy,
                )
            flat = w2_grouped[:].rearrange("p s m t -> p (s m t)")
            for first, sets in ((0, 8), (8, 4)):
                cols = slice(first * P, (first + sets) * P)
                nc.vector.quantize_mx(
                    out=w2_codes[:, cols].bitcast(FP8X4),
                    scales=w2_scales[:, cols],
                    in_=flat[:, first * K_PASS : (first + sets) * K_PASS],
                )

        prepare_second_stage()
        spread_small_operands()
        for i in range(PASSES + 2):
            if i < PASSES:
                for first in (0, 2, 4):
                    transpose_rows(i, first, nc.scalar.copy)
                if i < AS_LOADED:
                    load_behind(i)
            if 0 <= i - 1 < PASSES:
                quantise_pass(i - 1)
            ahead = i + SPLIT_AHEAD
            if AS_LOADED <= ahead < PASSES - 1:
                split_pass(ahead)
                load_behind(ahead)
            if 0 <= i - 2:
                multiply_pass(i - 2)

        hid_planes = consts.tile([P, HD_SETS, CLASSES], BF16)
        for t in range(HD_SETS):
            bias = bias_cols[:, B1_COL + t : B1_COL + t + 1]
            if t % 2 == 0:
                nc.scalar.activation(out=hid_planes[:, t, :], in_=hid_acc[t][:], func=ACT.Relu, bias=bias, scale=1.0)
            else:
                nc.vector.tensor_scalar(
                    out=hid_planes[:, t, :], in0=hid_acc[t][:], scalar1=bias, scalar2=0.0, op0=ALU.add, op1=ALU.max
                )
        hid_grouped = consts.tile([P, CLASSES, PACK], BF16, align_bytes=64)
        by_class = hid_planes[:].rearrange("p t c -> p c t")
        share = CLASSES * 3 // 4
        nc.vector.tensor_copy(out=hid_grouped[:, 0:share], in_=by_class[:, 0:share])
        nc.scalar.copy(out=hid_grouped[:, share:CLASSES], in_=by_class[:, share:CLASSES])
        hid_codes = consts.tile([P, CLASSES], U32, align_bytes=64)
        hid_scales = consts.tile([P, CLASSES], U8, align_bytes=64)
        nc.vector.quantize_mx(
            out=hid_codes[:].bitcast(FP8X4), scales=hid_scales[:], in_=hid_grouped[:].rearrange("p c t -> p (c t)")
        )

        out_rows = out.rearrange("(c p) x -> p c x", p=P)
        backs = []
        for i, (v, class_sets) in enumerate(((0, (0, 1)), (1, (0, 1)), (2, (0,)), (2, (1,)))):
            count = len(class_sets)
            back = accs.tile([P, count, 2, P], F32, name="back%d" % i, tag="acc%d" % i)
            w0_planes = w0_rows[:, v * 2 * P : (v + 1) * 2 * P].rearrange("p (m e) -> p e m", e=2)
            for n in range(count):
                nc.tensor.matmul(out=back[:, n], lhsT=ones[:], rhs=w0_planes, start=(n == 0), stop=False)
            backs.append((v, class_sets, back))

        products = {}

        def multiply_outputs(j):
            pre = banks.tile([P, 2, CLASSES], F32, tag="bank")
            for plane in range(2):
                outputs = slice((plane * E_SETS + j) * P, (plane * E_SETS + j + 1) * P)
                nc.tensor.matmul_mx(
                    out=pre[:, plane, :],
                    lhsT=w2_codes[:, outputs].bitcast(FP8X4),
                    lhsT_scale=w2_scales[:, outputs],
                    rhs=hid_codes[:].bitcast(FP8X4),
                    rhs_scale=hid_scales[:],
                    start=True,
                    stop=True,
                )
            gate = tail_pool.tile([P, CLASSES], F32)
            nc.scalar.activation(
                out=gate[:], in_=pre[:, 0, :], func=ACT.Sigmoid, bias=bias_cols[:, BGATE_COL + j : BGATE_COL + j + 1], scale=1.0
            )
            product = tail_pool.tile([P, CLASSES], F32)
            nc.vector.scalar_tensor_tensor(
                out=product[:],
                in0=pre[:, 1, :],
                scalar=bias_cols[:, BDW_COL + j : BDW_COL + j + 1],
                in1=gate[:],
                op0=ALU.add,
                op1=ALU.mult,
            )
            products[j] = product

        def turn_back(i):
            v, class_sets, back = backs[i]
            for n, c in enumerate(class_sets):
                for e in range(2):
                    nc.tensor.matmul(
                        out=back[:, n, e, :],
                        lhsT=products[2 * v + e][:, c * P : (c + 1) * P],
                        rhs=ident[:],
                        is_transpose=True,
                        start=False,
                        stop=(n == len(class_sets) - 1 and e == 1),
                    )

        def store(i):
            v, class_sets, back = backs[i]
            result = tail_pool.tile([P, len(class_sets), 2 * P], F32, name="result%d" % i, tag="result%d" % i, bufs=1)
            copy = nc.scalar.copy if i % 2 == 0 else nc.vector.tensor_copy
            copy(
                out=result[:].rearrange("p c (m e) -> p c m e", e=2), in_=back[:].rearrange("p c e m -> p c m e")
            )
            nc.sync.dma_start(
                out=out_rows[:, class_sets[0] : class_sets[-1] + 1, v * 2 * P : (v + 1) * 2 * P], in_=result[:]
            )

        for j in range(E_SETS):
            multiply_outputs(j)
        for i in range(len(backs)):
            turn_back(i)
            store(i)
